import numpy as np
import ml_dtypes


def mxq(x, axis, fmt="e4m3"):
    dtype, down = {"e4m3": (ml_dtypes.float8_e4m3fn, 7), "e5m2": (ml_dtypes.float8_e5m2, 14)}[fmt]
    v = np.moveaxis(np.asarray(x, np.float32).astype(ml_dtypes.bfloat16).astype(np.float64), axis, -1)
    blocks = v.reshape(v.shape[:-1] + (-1, 32))
    amax = np.abs(blocks).max(-1, keepdims=True)
    byte = np.maximum(np.where(amax > 0, np.frexp(amax)[1] - 1 + 127, 0) - down, 1)
    scale = np.exp2(byte - 127.0)
    codes = (blocks / scale).astype(np.float32).astype(dtype).astype(np.float64)
    return np.moveaxis((codes * scale).reshape(v.shape), -1, axis)


WIDE = False


def mx_kscale(k):
    if not WIDE:
        return np.ones(k)
    levels = np.array([18, -18])
    if k % 512:
        return np.exp2(np.random.permutation(np.resize(levels, k // 32))).repeat(32)
    a = np.empty((k // 512, 16))
    for p in range(k // 512):
        a[p, :8] = np.random.permutation(np.resize(levels, 8))
        for g in range(8):
            far = levels[np.abs(levels - a[p, g]) >= 10]
            a[p, g + 8] = far[np.random.randint(len(far))]
    return np.exp2(a.ravel()).repeat(32)


BF16 = ml_dtypes.bfloat16


def bf(x):
    return np.asarray(x, np.float32).astype(BF16)


def f64(x):
    return np.asarray(x).astype(np.float64)


B, L, E, H, HD, F, G = 4, 128, 1024, 8, 128, 2048, 2048
EPS = 1e-6
T, J = B * L, H * HD


def rope_diag():
    pair = np.arange(HD) // 2
    theta = 10000.0 ** (-2.0 * pair / HD)
    return np.cos(np.arange(L)[:, None] * theta[None, :])


def setup_inputs():
    s = mx_kscale(T)
    uq = mx_kscale(J).reshape(1, H, 1, HD)
    uk = mx_kscale(J).reshape(1, H, 1, HD)
    x0 = bf(np.random.standard_normal((B, L, E)))
    g = bf(1.0 + 0.1 * np.random.standard_normal(E))
    wq0 = bf(np.random.standard_normal((E, J)) / np.sqrt(E))
    wk0 = bf(np.random.standard_normal((E, J)) / np.sqrt(E))
    st = s.reshape(B, 1, L, 1)
    g0 = 2.0 * np.random.standard_normal((B, H, L, HD)) * np.exp2(np.random.randint(-6, 1, (B, 1, L, 1)))
    g1 = 2.0 * np.random.standard_normal((B, H, L, HD)) * np.exp2(np.random.randint(-6, 1, (B, 1, L, 1)))
    xf = f64(x0)
    rstd = 1.0 / np.sqrt(np.mean(xf * xf, axis=-1) + EPS)
    return {"x": bf(xf * s.reshape(B, L, 1)),
            "g": g,
            "wq": bf(f64(wq0) / uq.reshape(1, J)),
            "wk": bf(f64(wk0) / uk.reshape(1, J)),
            "rstd": np.asarray(rstd, np.float32),
            "grad_0": bf(g0 / st * uq),
            "grad_1": bf(g1 / st * uk)}


def reference(x, g, wq, wk, rstd, grad_0, grad_1):
    c = rope_diag()
    xf = f64(x).reshape(T, E)
    gf = f64(g)
    r = f64(rstd).reshape(T, 1)
    dq = (f64(grad_0) * c).transpose(0, 2, 1, 3).reshape(T, J)
    dk = (f64(grad_1) * c).transpose(0, 2, 1, 3).reshape(T, J)
    dz = np.concatenate([dq, dk], axis=1)
    w = np.concatenate([f64(wq), f64(wk)], axis=1)
    dh = mxq(dz, 1, "e5m2") @ mxq(w, 1, "e4m3").T
    h = xf * r * gf
    dw = mxq(h, 0, "e4m3").T @ mxq(dz, 0, "e5m2")
    a = gf * dh
    dx = r * a - xf * r ** 3 * np.mean(xf * a, axis=1, keepdims=True)
    return dx.reshape(B, L, E), dw[:, :J], dw[:, J:]

@@ -1,0 +1,325 @@
+import math
+from contextlib import ExitStack
+
+import concourse.mybir as mybir
+from concourse.masks import make_identity
+
+F32 = mybir.dt.float32
+BF16 = mybir.dt.bfloat16
+I32 = mybir.dt.int32
+U32 = mybir.dt.uint32
+U8 = mybir.dt.uint8
+E4M3 = mybir.dt.float8_e4m3fn_x4
+E5M2 = mybir.dt.float8_e5m2_x4
+ALU = mybir.AluOpType
+ACT = mybir.ActivationFunctionType
+
+P = 128
+B, L, E, NH, HD = 4, 128, 1024, 8, 128
+T = B * L
+J = NH * HD
+UNIT = 512
+HALF = 512
+FLOPS = 2 * 2 * T * E * 2 * J
+
+
+def R(h):
+    return [("R", h, j) for j in range(4)]
+
+
+def Z(u):
+    return [("Z", u, 0), ("Z", u, 1)]
+
+
+def W(u, h):
+    return [("W", u, h, 0), ("W", u, h, 1)]
+
+
+def weave(a, b):
+    out = []
+    for i in range(max(len(a), len(b))):
+        out.extend(a[i:i + 1])
+        out.extend(b[i:i + 1])
+    return out
+
+
+def tile_llamaselfattentionblock_pa_v_kernel(tc, x, g, wq, wk, rstd, grad_0, grad_1, out_0, out_1, out_2):
+    nc = tc.nc
+    grads = (grad_0, grad_1)
+    weights = (wq, wk)
+    outs = (out_1, out_2)
+    with ExitStack() as ctx:
+        keep = ctx.enter_context(tc.tile_pool(name="keep", bufs=1))
+        stage = ctx.enter_context(tc.tile_pool(name="stage", bufs=3))
+        psum = ctx.enter_context(tc.psum_pool(name="psum", bufs=1))
+
+        def kept(name, shape, dtype):
+            return keep.tile(shape, dtype, name=name, align_bytes=64)
+
+        r4 = kept("r4", [P, 4], F32)
+        grow = kept("grow", [P, E], BF16)
+        ones = kept("ones", [P, P], BF16)
+        ident = kept("ident", [P, P], F32)
+        xs = kept("xs", [P, 4, E], BF16)
+        gr = [kept("gr%d" % u, [P, 4, 4, HD], BF16) for u in range(4)]
+        wt = [[kept("wt%d%d" % (a, h), [P, 4, J], BF16) for h in range(2)] for a in range(2)]
+
+        ctx.enter_context(tc.manual_schedule())
+
+        nc.vector.memset(grow[:], 0.0)
+        nc.gpsimd.memset(ones[:], 1.0)
+        nc.sync.dma_start(out=r4[:], in_=rstd.rearrange("b (q j) -> (b q) j", j=4))
+        nc.sync.dma_start(out=grow[0:1, :], in_=g.rearrange("(o e) -> o e", o=1))
+
+        def load(name):
+            if name[0] == "G":
+                u = int(name[1])
+                for b in (0, 2, 1, 3):
+                    src = grads[u // 2][b, 4 * (u % 2):4 * (u % 2) + 4]
+                    nc.sync.dma_start(
+                        out=gr[u][32 * b:32 * b + 32].rearrange("q n j d -> q n (j d)"),
+                        in_=src.rearrange("n (q j) d -> q n (j d)", j=4))
+            if name[0] == "X":
+                h = int(name[1])
+                nc.sync.dma_start(
+                    out=xs[:, :, h * HALF:(h + 1) * HALF],
+                    in_=x.flatten_outer_dims().rearrange("(p j) e -> p j e", j=4)[:, :, h * HALF:(h + 1) * HALF])
+            if name[0] == "W":
+                a, h = int(name[1]), int(name[2])
+                nc.sync.dma_start(
+                    out=wt[a][h][:],
+                    in_=weights[a][h * HALF:(h + 1) * HALF, :].rearrange("(p i) f -> p i f", i=4))
+
+        for name in ("G0", "X0", "G1", "X1", "W00", "G2", "G3", "W10", "W01", "W11"):
+            load(name)
+
+        ints = kept("ints", [P, 4], I32)
+        pos = kept("pos", [P, 4], I32)
+        lt = kept("lt", [P, 4], F32)
+        coarse = kept("coarse", [P, 8], F32)
+        fine = kept("fine", [P, 8], F32)
+        theta = kept("theta", [P, 8, 8], F32)
+        turns = kept("turns", [P, 64, 4], F32)
+        whole = kept("whole", [P, 64, 4], I32)
+        part = kept("part", [P, 64, 4], F32)
+        cosines = kept("cosines", [P, 2, 32, 4], F32)
+        nc.gpsimd.iota(ints[:], pattern=[[1, 4]], base=0, channel_multiplier=4)
+        make_identity(nc, ident[:])
+        nc.vector.memset(coarse[:], 1.0)
+        nc.vector.memset(fine[:], 1.0)
+        for s in (1, 2, 4):
+            nc.vector.tensor_single_scalar(coarse[:, s:2 * s], coarse[:, 0:s], 10000.0 ** (-s / 8.0), ALU.mult)
+            nc.vector.tensor_single_scalar(fine[:, s:2 * s], fine[:, 0:s], 10000.0 ** (-s / 64.0), ALU.mult)
+        nc.vector.tensor_single_scalar(pos[:], ints[:], L - 1, ALU.bitwise_and)
+        nc.vector.tensor_tensor(theta[:], coarse[:].unsqueeze(2).to_broadcast([P, 8, 8]),
+                                fine[:].unsqueeze(1).to_broadcast([P, 8, 8]), ALU.mult)
+        nc.vector.tensor_single_scalar(lt[:], pos[:], 0.5 / math.pi, ALU.mult)
+        nc.vector.tensor_tensor(turns[:], theta[:].rearrange("p a b -> p (a b)").unsqueeze(2).to_broadcast([P, 64, 4]),
+                                lt[:].unsqueeze(1).to_broadcast([P, 64, 4]), ALU.mult)
+        nc.vector.tensor_single_scalar(whole[:], turns[:], 0.25, ALU.add)
+        nc.vector.scalar_tensor_tensor(part[:].rearrange("p i j -> p (i j)"), turns[:].rearrange("p i j -> p (i j)"), 0.25,
+                                       whole[:].rearrange("p i j -> p (i j)"), ALU.add, ALU.subtract)
+        nc.scalar.activation(out=cosines[:], in_=part[:].rearrange("p (m t) j -> p t m j", t=2),
+                             func=ACT.Sin, scale=2.0 * math.pi)
+        nr2 = kept("nr2", [P, 4], F32)
+        nc.vector.scalar_tensor_tensor(nr2[:], r4[:], -1.0 / E, r4[:], ALU.mult, ALU.mult)
+
+        rg = kept("rg", [P, 4, E], F32)
+        gps = []
+        for h in range(2):
+            bank = psum.tile([P, HALF], F32, name="gps%d" % h, tag="dh", bufs=2)
+            nc.tensor.matmul(bank[:], lhsT=ones[:], rhs=grow[:, h * HALF:(h + 1) * HALF], start=True, stop=True)
+            gps.append(bank)
+        cps = psum.tile([P, 2, 32, 8], F32, name="cps", tag="dw", bufs=3)
+        cos_bank = cps[:].rearrange("p t m j -> p (t m j)")[:, 0:256]
+        nc.tensor.matmul(cos_bank, lhsT=ident[:], rhs=cosines[:].rearrange("p t m j -> p (t m j)"), start=True, stop=True)
+        cos4 = cos_bank.rearrange("p (t m j) -> p t m j", t=2, j=4)
+
+        dz = [kept("dz%d" % u, [P, UNIT, 4], BF16) for u in range(4)]
+        zt = [kept("zt%d" % u, [P, 4, P, 4], BF16) for u in range(4)]
+        ht = [kept("ht%d" % h, [P, HALF, 4], BF16) for h in range(2)]
+        wg = {}
+
+        def codes(name):
+            return kept(name + "_codes", [P, 512], U32), kept(name + "_scales", [P, 512], U8)
+
+        dzq = [codes("dzq%d" % u) for u in range(4)]
+        ztq = [codes("ztq%d" % u) for u in range(4)]
+        htq = [codes("htq%d" % h) for h in range(2)]
+        wgq = [[codes("wgq%d%d" % (u, h)) for h in range(2)] for u in range(4)]
+        ra = [kept("ra%d" % j, [P, E], F32) for j in range(4)]
+        coef = [kept("coef%d" % j, [P, 1], F32) for j in range(4)]
+
+        def rope(u):
+            for t in range(4):
+                nc.vector.tensor_tensor(
+                    out=dz[u][:, t * P:(t + 1) * P, :].rearrange("p (n m) j -> p n m j", n=4),
+                    in0=gr[u][:, :, :, t:HD:4].rearrange("p n j m -> p n m j"),
+                    in1=cos4[:, t // 2].unsqueeze(1).to_broadcast([P, 4, 32, 4]),
+                    op=ALU.mult)
+
+        def quantize(pair, dtype, src):
+            nc.vector.quantize_mx(out=pair[0][:].bitcast(dtype), scales=pair[1][:], in_=src)
+
+        def normed(h):
+            for c in range(2):
+                cols = slice(h * HALF + 256 * c, h * HALF + 256 * (c + 1))
+                nc.gpsimd.tensor_tensor(out=ht[h][:, 256 * c:256 * (c + 1), :], in0=xs[:, :, cols].rearrange("p j e -> p e j"),
+                                        in1=rg[:, :, cols].rearrange("p j e -> p e j"), op=ALU.mult)
+
+        banks = {}
+
+        def pe(b):
+            k = b[0]
+            if k == "Z":
+                u, jp = b[1:]
+                bank = psum.tile([P, 4, P], F32, name="tr", tag="tr", bufs=3)
+                words = dz[u][:].rearrange("p c j -> p (c j)").bitcast(F32)
+                for t in range(4):
+                    nc.tensor.transpose(bank[:, t, :], words[:, 2 * P * t + jp:2 * P * (t + 1):2], ident[:])
+            elif k == "W":
+                u, h, ip = b[1:]
+                bank = psum.tile([P, 4, P], F32, name="tr", tag="tr", bufs=3)
+                words = wt[u // 2][h][:].rearrange("p i f -> p (i f)").bitcast(F32)
+                for i2 in range(2):
+                    for ul in range(2):
+                        w0 = (2 * ip + i2) * (J // 2) + (u % 2) * (UNIT // 2)
+                        nc.tensor.transpose(bank[:, 2 * i2 + ul, :], words[:, w0 + ul:w0 + UNIT // 2:2], ident[:])
+            else:
+                u, e = b[1:]
+                bank = psum.tile([P, UNIT], F32, name="dw", tag="dw", bufs=3)
+                hc, hs = htq[e // 4]
+                cols = slice((e % 4) * P, (e % 4 + 1) * P)
+                nc.tensor.matmul_mx(out=bank[:], lhsT=hc[:, cols].bitcast(E4M3), lhsT_scale=hs[:, cols],
+                                    rhs=dzq[u][0][:].bitcast(E5M2), rhs_scale=dzq[u][1][:], start=True, stop=True)
+            banks[b] = bank
+
+        def copy(engine, out, in_):
+            if engine == "V":
+                nc.vector.tensor_copy(out=out, in_=in_)
+            else:
+                nc.scalar.copy(out=out, in_=in_)
+
+        def drain(b, engine):
+            k = b[0]
+            if k == "R":
+                h, j = b[1:]
+                nc.scalar.activation(out=rg[:, j, h * HALF:(h + 1) * HALF], in_=gps[h][:], func=ACT.Copy, scale=r4[:, j:j + 1])
+                return
+            bank = banks.pop(b)
+            if k == "Z":
+                u, jp = b[1:]
+                copy(engine, zt[u][:, 2 * jp:2 * jp + 2],
+                     bank[:].rearrange("p t q -> p (t q)").bitcast(BF16).rearrange("p (t q e) -> p e q t", t=4, e=2))
+            elif k == "W":
+                u, h, ip = b[1:]
+                if (u, h) not in wg:
+                    wg[(u, h)] = stage.tile([P, HALF, 4], BF16, name="wg", tag="wg", bufs=4, align_bytes=64)
+                dst = wg[(u, h)][:].rearrange("p c t -> p (c t)").bitcast(F32).rearrange("p (q w) -> p q w", w=8)
+                copy(engine, dst[:, :, 4 * ip:4 * ip + 4], bank[:].rearrange("p c q -> p q c"))
+            else:
+                u, e = b[1:]
+                st = stage.tile([P, UNIT], F32, name="st", tag="st", bufs=8)
+                copy(engine, st[:].rearrange("p (m t) -> p m t", t=4), bank[:].rearrange("p (t m) -> p m t", t=4))
+                nc.sync.dma_start(out=outs[u // 2][e * P:(e + 1) * P, (u % 2) * UNIT:(u % 2 + 1) * UNIT], in_=st[:])
+
+        dhb = {}
+
+        def dh(j, h):
+            bank = psum.tile([P, HALF], F32, name="dh", tag="dh", bufs=2)
+            cols = slice(j * P, (j + 1) * P)
+            for u in range(4):
+                nc.tensor.matmul_mx(out=bank[:], lhsT=ztq[u][0][:, cols].bitcast(E5M2), lhsT_scale=ztq[u][1][:, cols],
+                                    rhs=wgq[u][h][0][:].bitcast(E4M3), rhs_scale=wgq[u][h][1][:],
+                                    start=(u == 0), stop=(u == 3))
+            dhb[(j, h)] = bank
+
+        def s1(j, h):
+            cols = slice(h * HALF, (h + 1) * HALF)
+            nc.vector.tensor_tensor(out=ra[j][:, cols], in0=dhb[(j, h)][:], in1=rg[:, j, cols], op=ALU.mult)
+
+        def s2(j):
+            junk = stage.tile([P, E], F32, name="junk", tag="junk", bufs=2)
+            nc.vector.scalar_tensor_tensor(junk[:], xs[:, j, :], nr2[:, j:j + 1], ra[j][:], ALU.mult, ALU.mult, accum_out=coef[j][:])
+
+        def s3(j):
+            res = stage.tile([P, E], F32, name="res", tag="res", bufs=2)
+            nc.vector.scalar_tensor_tensor(res[:], xs[:, j, :], coef[j][:], ra[j][:], ALU.mult, ALU.add)
+            nc.sync.dma_start(out=out_0.flatten_outer_dims().rearrange("(p j) e -> p j e", j=4)[:, j, :], in_=res[:])
+
+        vector = [("h", 0), ("rope", 0), ("rope", 1), ("rope", 2), ("qz", 0), ("qh", 0), ("h", 1), ("rope", 3), ("qt", 0), ("qz", 1), ("qw", 0, 0),
+                  ("qt", 1), ("qz", 2), ("qw", 1, 0), ("qh", 1), ("qt", 2), ("qz", 3), ("qw", 2, 0), ("qt", 3), ("qw", 3, 0),
+                  ("qw", 0, 1), ("qw", 1, 1), ("qw", 2, 1), ("qw", 3, 1),
+                  ("dh", 0, 0), ("dh", 0, 1), ("s1", 0, 0), ("s1", 0, 1), ("dh", 1, 0), ("dh", 1, 1), ("s1", 1, 0), ("s2", 0), ("s1", 1, 1),
+                  ("dh", 2, 0), ("dh", 2, 1), ("s3", 0), ("s1", 2, 0), ("s2", 1), ("s1", 2, 1), ("dh", 3, 0), ("dh", 3, 1), ("s3", 1),
+                  ("s1", 3, 0), ("s2", 2), ("s1", 3, 1), ("s3", 2), ("s2", 3), ("s3", 3)]
+        dws = [("D", u, e) for u in range(4) for e in range(8)]
+        behind = (R(0) + R(1) + Z(0) + Z(1) + W(0, 0) + Z(2) + dws[0:1] + W(1, 0) + Z(3) + W(2, 0) + W(3, 0)
+                  + W(0, 1) + dws[1:4] + W(1, 1) + dws[4:7] + W(2, 1) + dws[7:10] + W(3, 1) + dws[10:])
+        on_vector = [("W", 2, 0, 1), ("W", 3, 0, 1)] + [("W", u, 1, 1) for u in range(4)]
+        pace = {"rope": 1, "h": 0, "qz": 2, "qh": 2, "qt": 2, "qw": 2, "s1": 1, "s2": 1, "s3": 1, "dh": 0}
+        look = 1
+        pos_pe = [0]
+        pos_s = [0]
+        made = set()
+
+        def can_pe(b):
+            if b[0] == "R":
+                return True
+            waiting = [c for c in behind[pos_s[0]:pos_pe[0]] if c[0] != "R" and (c[0] == "D") == (b[0] == "D")]
+            if len(waiting) >= 3:
+                return False
+            if b[0] == "Z":
+                return ("rope", b[1]) in made
+            if b[0] == "D":
+                return ("qz", b[1]) in made and ("qh", b[2] // 4) in made
+            return True
+
+        def pump(n):
+            for i in range(n):
+                if pos_s[0] >= len(behind):
+                    return
+                while pos_pe[0] < min(len(behind), pos_s[0] + 1 + look) and can_pe(behind[pos_pe[0]]):
+                    if behind[pos_pe[0]][0] != "R":
+                        pe(behind[pos_pe[0]])
+                    pos_pe[0] += 1
+                if pos_pe[0] <= pos_s[0]:
+                    return
+                drain(behind[pos_s[0]], "V" if behind[pos_s[0]] in on_vector else "S")
+                pos_s[0] += 1
+
+        def need(kind, *key):
+            while any(b[0] == kind and b[1:1 + len(key)] == key for b in behind[pos_s[0]:]):
+                before = pos_s[0]
+                pump(1)
+                assert pos_s[0] > before, "stuck"
+
+        for v in vector:
+            k = v[0]
+            if k == "rope":
+                rope(v[1])
+            elif k == "h":
+                need("R", v[1])
+                normed(v[1])
+            elif k == "qz":
+                quantize(dzq[v[1]], E5M2, dz[v[1]][:].rearrange("p c j -> p (c j)"))
+            elif k == "qh":
+                quantize(htq[v[1]], E4M3, ht[v[1]][:].rearrange("p c j -> p (c j)"))
+            elif k == "qt":
+                need("Z", v[1])
+                quantize(ztq[v[1]], E5M2, zt[v[1]][:].rearrange("p j q t -> p (j q t)"))
+            elif k == "qw":
+                need("W", v[1], v[2])
+                quantize(wgq[v[1]][v[2]], E4M3, wg[(v[1], v[2])][:].rearrange("p c t -> p (c t)"))
+            elif k == "dh":
+                dh(v[1], v[2])
+            elif k == "s1":
+                s1(v[1], v[2])
+            elif k == "s2":
+                s2(v[1])
+            else:
+                s3(v[1])
+            made.add(v)
+            pump(pace[k])
+        while pos_s[0] < len(behind):
+            pump(1)

@@ -35,14 +35,6 @@ def W(u, h):
     return [("W", u, h, 0), ("W", u, h, 1)]
 
 
-def weave(a, b):
-    out = []
-    for i in range(max(len(a), len(b))):
-        out.extend(a[i:i + 1])
-        out.extend(b[i:i + 1])
-    return out
-
-
 def tile_llamaselfattentionblock_pa_v_kernel(tc, x, g, wq, wk, rstd, grad_0, grad_1, out_0, out_1, out_2):
     nc = tc.nc
     grads = (grad_0, grad_1)
@@ -61,7 +53,7 @@ def tile_llamaselfattentionblock_pa_v_kernel(tc, x, g, wq, wk, rstd, grad_0, gra
         ones = kept("ones", [P, P], BF16)
         ident = kept("ident", [P, P], F32)
         xs = kept("xs", [P, 4, E], BF16)
-        gr = [kept("gr%d" % u, [P, 4, 4, HD], BF16) for u in range(4)]
+        gr = [kept("gr%d" % a, [P, NH, 4, HD], BF16) for a in range(2)]
         wt = [[kept("wt%d%d" % (a, h), [P, 4, J], BF16) for h in range(2)] for a in range(2)]
 
         ctx.enter_context(tc.manual_schedule())
@@ -72,13 +64,6 @@ def tile_llamaselfattentionblock_pa_v_kernel(tc, x, g, wq, wk, rstd, grad_0, gra
         nc.sync.dma_start(out=grow[0:1, :], in_=g.rearrange("(o e) -> o e", o=1))
 
         def load(name):
-            if name[0] == "G":
-                u = int(name[1])
-                for b in (0, 2, 1, 3):
-                    src = grads[u // 2][b, 4 * (u % 2):4 * (u % 2) + 4]
-                    nc.sync.dma_start(
-                        out=gr[u][32 * b:32 * b + 32].rearrange("q n j d -> q n (j d)"),
-                        in_=src.rearrange("n (q j) d -> q n (j d)", j=4))
             if name[0] == "X":
                 h = int(name[1])
                 nc.sync.dma_start(
@@ -90,7 +75,18 @@ def tile_llamaselfattentionblock_pa_v_kernel(tc, x, g, wq, wk, rstd, grad_0, gra
                     out=wt[a][h][:],
                     in_=weights[a][h * HALF:(h + 1) * HALF, :].rearrange("(p i) f -> p i f", i=4))
 
-        for name in ("G0", "X0", "G1", "X1", "W00", "G2", "G3", "W10", "W01", "W11"):
+        def load_grad(a, b):
+            queue = nc.sync if b < 2 else nc.scalar
+            queue.dma_start(out=gr[a][32 * b:32 * b + 32].rearrange("q n j d -> q n (j d)"),
+                            in_=grads[a][b].rearrange("n (q j) d -> q n (j d)", j=4))
+
+        for b in (0, 2, 1, 3):
+            load_grad(0, b)
+        for name in ("X0", "X1"):
+            load(name)
+        load_grad(1, 0)
+        load_grad(1, 1)
+        for name in ("W00", "W10", "W01", "W11"):
             load(name)
 
         ints = kept("ints", [P, 4], I32)
@@ -127,12 +123,14 @@ def tile_llamaselfattentionblock_pa_v_kernel(tc, x, g, wq, wk, rstd, grad_0, gra
         rg = kept("rg", [P, 4, E], F32)
         gps = []
         for h in range(2):
-            bank = psum.tile([P, HALF], F32, name="gps%d" % h, tag="dh", bufs=2)
+            bank = psum.tile([P, HALF], F32, name="gps%d" % h, tag="tr", bufs=3)
             nc.tensor.matmul(bank[:], lhsT=ones[:], rhs=grow[:, h * HALF:(h + 1) * HALF], start=True, stop=True)
             gps.append(bank)
         cps = psum.tile([P, 2, 32, 8], F32, name="cps", tag="dw", bufs=3)
         cos_bank = cps[:].rearrange("p t m j -> p (t m j)")[:, 0:256]
         nc.tensor.matmul(cos_bank, lhsT=ident[:], rhs=cosines[:].rearrange("p t m j -> p (t m j)"), start=True, stop=True)
+        warm = psum.tile([P, HALF], F32, name="warm", tag="dh", bufs=2)
+        load_grad(1, 2)
         cos4 = cos_bank.rearrange("p (t m j) -> p t m j", t=2, j=4)
 
         dz = [kept("dz%d" % u, [P, UNIT, 4], BF16) for u in range(4)]
@@ -154,7 +152,7 @@ def tile_llamaselfattentionblock_pa_v_kernel(tc, x, g, wq, wk, rstd, grad_0, gra
             for t in range(4):
                 nc.vector.tensor_tensor(
                     out=dz[u][:, t * P:(t + 1) * P, :].rearrange("p (n m) j -> p n m j", n=4),
-                    in0=gr[u][:, :, :, t:HD:4].rearrange("p n j m -> p n m j"),
+                    in0=gr[u // 2][:, 4 * (u % 2):4 * (u % 2) + 4, :, t:HD:4].rearrange("p n j m -> p n m j"),
                     in1=cos4[:, t // 2].unsqueeze(1).to_broadcast([P, 4, 32, 4]),
                     op=ALU.mult)
 
@@ -171,6 +169,9 @@ def tile_llamaselfattentionblock_pa_v_kernel(tc, x, g, wq, wk, rstd, grad_0, gra
 
         def pe(b):
             k = b[0]
+            if k == "M":
+                nc.tensor.matmul(warm[:], lhsT=ones[:], rhs=grow[:, 0:HALF], start=True, stop=True)
+                return
             if k == "Z":
                 u, jp = b[1:]
                 bank = psum.tile([P, 4, P], F32, name="tr", tag="tr", bufs=3)
@@ -202,9 +203,13 @@ def tile_llamaselfattentionblock_pa_v_kernel(tc, x, g, wq, wk, rstd, grad_0, gra
 
         def drain(b, engine):
             k = b[0]
+            if k == "M":
+                return
             if k == "R":
                 h, j = b[1:]
                 nc.scalar.activation(out=rg[:, j, h * HALF:(h + 1) * HALF], in_=gps[h][:], func=ACT.Copy, scale=r4[:, j:j + 1])
+                if (h, j) == (0, 0):
+                    load_grad(1, 3)
                 return
             bank = banks.pop(b)
             if k == "Z":
@@ -254,19 +259,26 @@ def tile_llamaselfattentionblock_pa_v_kernel(tc, x, g, wq, wk, rstd, grad_0, gra
                   ("dh", 2, 0), ("dh", 2, 1), ("s3", 0), ("s1", 2, 0), ("s2", 1), ("s1", 2, 1), ("dh", 3, 0), ("dh", 3, 1), ("s3", 1),
                   ("s1", 3, 0), ("s2", 2), ("s1", 3, 1), ("s3", 2), ("s2", 3), ("s3", 3)]
         dws = [("D", u, e) for u in range(4) for e in range(8)]
-        behind = (R(0) + R(1) + Z(0) + Z(1) + W(0, 0) + Z(2) + dws[0:1] + W(1, 0) + Z(3) + W(2, 0) + W(3, 0)
-                  + W(0, 1) + dws[1:4] + W(1, 1) + dws[4:7] + W(2, 1) + dws[7:10] + W(3, 1) + dws[10:])
-        on_vector = [("W", 2, 0, 1), ("W", 3, 0, 1)] + [("W", u, 1, 1) for u in range(4)]
-        pace = {"rope": 1, "h": 0, "qz": 2, "qh": 2, "qt": 2, "qw": 2, "s1": 1, "s2": 1, "s3": 1, "dh": 0}
-        look = 1
+        pairs = [Z(0), Z(1), W(0, 0), Z(2), W(1, 0), Z(3), W(2, 0), W(3, 0), W(0, 1), W(1, 1), W(2, 1), W(3, 1)]
+        products = (0, 0, 1, 1, 1, 0, 1, 1, 3, 3, 3, 2)
+        M = [("M",)]
+        behind = M * 4 + R(0) + R(1)
+        given = 0
+        for pair, n in zip(pairs, products):
+            behind = behind + pair + dws[given:given + n] + M * (2 - n)
+            given += n
+        behind = behind + dws[given:]
+        on_vector = [("Z", 2, 1), ("Z", 3, 1)] + [("W", u, 1, 1) for u in range(4)]
+        pace = {"rope": 3, "h": 0, "qz": 1, "qh": 1, "qt": 1, "qw": 1, "s1": 1, "s2": 1, "s3": 1, "dh": 0}
+        look = 2
         pos_pe = [0]
         pos_s = [0]
         made = set()
 
         def can_pe(b):
-            if b[0] == "R":
+            if b[0] in ("R", "M"):
                 return True
-            waiting = [c for c in behind[pos_s[0]:pos_pe[0]] if c[0] != "R" and (c[0] == "D") == (b[0] == "D")]
+            waiting = [c for c in behind[pos_s[0]:pos_pe[0]] if c[0] not in ("R", "M") and (c[0] == "D") == (b[0] == "D")]
             if len(waiting) >= 3:
                 return False
             if b[0] == "Z":
@@ -287,6 +299,8 @@ def tile_llamaselfattentionblock_pa_v_kernel(tc, x, g, wq, wk, rstd, grad_0, gra
                     return
                 drain(behind[pos_s[0]], "V" if behind[pos_s[0]] in on_vector else "S")
                 pos_s[0] += 1
+                while pos_s[0] < pos_pe[0] and behind[pos_s[0]][0] == "M":
+                    pos_s[0] += 1
 
         def need(kind, *key):
             while any(b[0] == kind and b[1:1 + len(key)] == key for b in behind[pos_s[0]:]):

@@ -75,18 +75,18 @@ def tile_llamaselfattentionblock_pa_v_kernel(tc, x, g, wq, wk, rstd, grad_0, gra
                     out=wt[a][h][:],
                     in_=weights[a][h * HALF:(h + 1) * HALF, :].rearrange("(p i) f -> p i f", i=4))
 
-        def load_grad(a, b):
+        def load_grad(a, b, n0, n1):
             queue = nc.sync if b < 2 else nc.scalar
-            queue.dma_start(out=gr[a][32 * b:32 * b + 32].rearrange("q n j d -> q n (j d)"),
-                            in_=grads[a][b].rearrange("n (q j) d -> q n (j d)", j=4))
+            queue.dma_start(out=gr[a][32 * b:32 * b + 32, n0:n1].rearrange("q n j d -> q n (j d)"),
+                            in_=grads[a][b, n0:n1].rearrange("n (q j) d -> q n (j d)", j=4))
 
-        for b in (0, 2, 1, 3):
-            load_grad(0, b)
-        for name in ("X0", "X1"):
-            load(name)
-        load_grad(1, 0)
-        load_grad(1, 1)
-        for name in ("W00", "W10", "W01", "W11"):
+        for n0 in (0, 4):
+            for b in (0, 2, 1, 3):
+                load_grad(0, b, n0, n0 + 4)
+        load("X0")
+        load_grad(1, 0, 0, 8)
+        load_grad(1, 1, 0, 8)
+        for name in ("W00", "X1", "W10", "W01", "W11"):
             load(name)
 
         ints = kept("ints", [P, 4], I32)
@@ -95,10 +95,10 @@ def tile_llamaselfattentionblock_pa_v_kernel(tc, x, g, wq, wk, rstd, grad_0, gra
         coarse = kept("coarse", [P, 8], F32)
         fine = kept("fine", [P, 8], F32)
         theta = kept("theta", [P, 8, 8], F32)
-        turns = kept("turns", [P, 64, 4], F32)
-        whole = kept("whole", [P, 64, 4], I32)
-        part = kept("part", [P, 64, 4], F32)
-        cosines = kept("cosines", [P, 2, 32, 4], F32)
+        turns = kept("turns", [P, 4, 64], F32)
+        whole = kept("whole", [P, 4, 64], I32)
+        part = kept("part", [P, 4, 64], F32)
+        cosines = kept("cosines", [P, 4, HD], F32)
         nc.gpsimd.iota(ints[:], pattern=[[1, 4]], base=0, channel_multiplier=4)
         make_identity(nc, ident[:])
         nc.vector.memset(coarse[:], 1.0)
@@ -110,12 +110,13 @@ def tile_llamaselfattentionblock_pa_v_kernel(tc, x, g, wq, wk, rstd, grad_0, gra
         nc.vector.tensor_tensor(theta[:], coarse[:].unsqueeze(2).to_broadcast([P, 8, 8]),
                                 fine[:].unsqueeze(1).to_broadcast([P, 8, 8]), ALU.mult)
         nc.vector.tensor_single_scalar(lt[:], pos[:], 0.5 / math.pi, ALU.mult)
-        nc.vector.tensor_tensor(turns[:], theta[:].rearrange("p a b -> p (a b)").unsqueeze(2).to_broadcast([P, 64, 4]),
-                                lt[:].unsqueeze(1).to_broadcast([P, 64, 4]), ALU.mult)
+        nc.vector.tensor_tensor(turns[:], theta[:].rearrange("p a b -> p (a b)").unsqueeze(1).to_broadcast([P, 4, 64]),
+                                lt[:].unsqueeze(2).to_broadcast([P, 4, 64]), ALU.mult)
         nc.vector.tensor_single_scalar(whole[:], turns[:], 0.25, ALU.add)
-        nc.vector.scalar_tensor_tensor(part[:].rearrange("p i j -> p (i j)"), turns[:].rearrange("p i j -> p (i j)"), 0.25,
-                                       whole[:].rearrange("p i j -> p (i j)"), ALU.add, ALU.subtract)
-        nc.scalar.activation(out=cosines[:], in_=part[:].rearrange("p (m t) j -> p t m j", t=2),
+        nc.vector.scalar_tensor_tensor(part[:].rearrange("p j i -> p (j i)"), turns[:].rearrange("p j i -> p (j i)"), 0.25,
+                                       whole[:].rearrange("p j i -> p (j i)"), ALU.add, ALU.subtract)
+        nc.scalar.activation(out=cosines[:].rearrange("p j (i s) -> p (j i) s", s=2),
+                             in_=part[:].rearrange("p j i -> p (j i)").unsqueeze(2).to_broadcast([P, 256, 2]),
                              func=ACT.Sin, scale=2.0 * math.pi)
         nr2 = kept("nr2", [P, 4], F32)
         nc.vector.scalar_tensor_tensor(nr2[:], r4[:], -1.0 / E, r4[:], ALU.mult, ALU.mult)
@@ -126,12 +127,8 @@ def tile_llamaselfattentionblock_pa_v_kernel(tc, x, g, wq, wk, rstd, grad_0, gra
             bank = psum.tile([P, HALF], F32, name="gps%d" % h, tag="tr", bufs=3)
             nc.tensor.matmul(bank[:], lhsT=ones[:], rhs=grow[:, h * HALF:(h + 1) * HALF], start=True, stop=True)
             gps.append(bank)
-        cps = psum.tile([P, 2, 32, 8], F32, name="cps", tag="dw", bufs=3)
-        cos_bank = cps[:].rearrange("p t m j -> p (t m j)")[:, 0:256]
-        nc.tensor.matmul(cos_bank, lhsT=ident[:], rhs=cosines[:].rearrange("p t m j -> p (t m j)"), start=True, stop=True)
         warm = psum.tile([P, HALF], F32, name="warm", tag="dh", bufs=2)
-        load_grad(1, 2)
-        cos4 = cos_bank.rearrange("p (t m j) -> p t m j", t=2, j=4)
+        load_grad(1, 2, 0, 8)
 
         dz = [kept("dz%d" % u, [P, UNIT, 4], BF16) for u in range(4)]
         zt = [kept("zt%d" % u, [P, 4, P, 4], BF16) for u in range(4)]
@@ -149,11 +146,11 @@ def tile_llamaselfattentionblock_pa_v_kernel(tc, x, g, wq, wk, rstd, grad_0, gra
         coef = [kept("coef%d" % j, [P, 1], F32) for j in range(4)]
 
         def rope(u):
-            for t in range(4):
+            for n in range(4):
                 nc.vector.tensor_tensor(
-                    out=dz[u][:, t * P:(t + 1) * P, :].rearrange("p (n m) j -> p n m j", n=4),
-                    in0=gr[u // 2][:, 4 * (u % 2):4 * (u % 2) + 4, :, t:HD:4].rearrange("p n j m -> p n m j"),
-                    in1=cos4[:, t // 2].unsqueeze(1).to_broadcast([P, 4, 32, 4]),
+                    out=dz[u][:, n * HD:(n + 1) * HD, :].rearrange("p (c i) j -> p c j i", i=4),
+                    in0=gr[u // 2][:, 4 * (u % 2) + n].rearrange("p j (c i) -> p c j i", i=4),
+                    in1=cosines[:].rearrange("p j (c i) -> p c j i", i=4),
                     op=ALU.mult)
 
         def quantize(pair, dtype, src):
@@ -162,8 +159,10 @@ def tile_llamaselfattentionblock_pa_v_kernel(tc, x, g, wq, wk, rstd, grad_0, gra
         def normed(h):
             for c in range(2):
                 cols = slice(h * HALF + 256 * c, h * HALF + 256 * (c + 1))
-                nc.gpsimd.tensor_tensor(out=ht[h][:, 256 * c:256 * (c + 1), :], in0=xs[:, :, cols].rearrange("p j e -> p e j"),
-                                        in1=rg[:, :, cols].rearrange("p j e -> p e j"), op=ALU.mult)
+                nc.vector.tensor_tensor(
+                    out=ht[h][:, 256 * c:256 * (c + 1), :].rearrange("p (c i) j -> p c j i", i=4),
+                    in0=xs[:, :, cols].rearrange("p j (c i) -> p c j i", i=4),
+                    in1=rg[:, :, cols].rearrange("p j (c i) -> p c j i", i=4), op=ALU.mult)
 
         banks = {}
 
@@ -177,7 +176,7 @@ def tile_llamaselfattentionblock_pa_v_kernel(tc, x, g, wq, wk, rstd, grad_0, gra
                 bank = psum.tile([P, 4, P], F32, name="tr", tag="tr", bufs=3)
                 words = dz[u][:].rearrange("p c j -> p (c j)").bitcast(F32)
                 for t in range(4):
-                    nc.tensor.transpose(bank[:, t, :], words[:, 2 * P * t + jp:2 * P * (t + 1):2], ident[:])
+                    nc.tensor.transpose(bank[:, t, :], words[:, 2 * t + jp:2 * UNIT:8], ident[:])
             elif k == "W":
                 u, h, ip = b[1:]
                 bank = psum.tile([P, 4, P], F32, name="tr", tag="tr", bufs=3)
@@ -209,7 +208,7 @@ def tile_llamaselfattentionblock_pa_v_kernel(tc, x, g, wq, wk, rstd, grad_0, gra
                 h, j = b[1:]
                 nc.scalar.activation(out=rg[:, j, h * HALF:(h + 1) * HALF], in_=gps[h][:], func=ACT.Copy, scale=r4[:, j:j + 1])
                 if (h, j) == (0, 0):
-                    load_grad(1, 3)
+                    load_grad(1, 3, 0, 8)
                 return
             bank = banks.pop(b)
             if k == "Z":
@@ -225,7 +224,7 @@ def tile_llamaselfattentionblock_pa_v_kernel(tc, x, g, wq, wk, rstd, grad_0, gra
             else:
                 u, e = b[1:]
                 st = stage.tile([P, UNIT], F32, name="st", tag="st", bufs=8)
-                copy(engine, st[:].rearrange("p (m t) -> p m t", t=4), bank[:].rearrange("p (t m) -> p m t", t=4))
+                copy(engine, st[:], bank[:])
                 nc.sync.dma_start(out=outs[u // 2][e * P:(e + 1) * P, (u % 2) * UNIT:(u % 2 + 1) * UNIT], in_=st[:])
 
         dhb = {}
@@ -252,24 +251,24 @@ def tile_llamaselfattentionblock_pa_v_kernel(tc, x, g, wq, wk, rstd, grad_0, gra
             nc.vector.scalar_tensor_tensor(res[:], xs[:, j, :], coef[j][:], ra[j][:], ALU.mult, ALU.add)
             nc.sync.dma_start(out=out_0.flatten_outer_dims().rearrange("(p j) e -> p j e", j=4)[:, j, :], in_=res[:])
 
-        vector = [("h", 0), ("rope", 0), ("rope", 1), ("rope", 2), ("qz", 0), ("qh", 0), ("h", 1), ("rope", 3), ("qt", 0), ("qz", 1), ("qw", 0, 0),
-                  ("qt", 1), ("qz", 2), ("qw", 1, 0), ("qh", 1), ("qt", 2), ("qz", 3), ("qw", 2, 0), ("qt", 3), ("qw", 3, 0),
+        vector = [("rope", 0), ("rope", 1), ("rope", 2), ("rope", 3), ("h", 0), ("qz", 0), ("h", 1), ("qh", 0), ("qz", 1), ("qt", 0), ("qz", 2),
+                  ("qh", 1), ("qw", 0, 0), ("qt", 1), ("qz", 3), ("qw", 1, 0), ("qt", 2), ("qw", 2, 0), ("qt", 3), ("qw", 3, 0),
                   ("qw", 0, 1), ("qw", 1, 1), ("qw", 2, 1), ("qw", 3, 1),
                   ("dh", 0, 0), ("dh", 0, 1), ("s1", 0, 0), ("s1", 0, 1), ("dh", 1, 0), ("dh", 1, 1), ("s1", 1, 0), ("s2", 0), ("s1", 1, 1),
                   ("dh", 2, 0), ("dh", 2, 1), ("s3", 0), ("s1", 2, 0), ("s2", 1), ("s1", 2, 1), ("dh", 3, 0), ("dh", 3, 1), ("s3", 1),
                   ("s1", 3, 0), ("s2", 2), ("s1", 3, 1), ("s3", 2), ("s2", 3), ("s3", 3)]
         dws = [("D", u, e) for u in range(4) for e in range(8)]
-        pairs = [Z(0), Z(1), W(0, 0), Z(2), W(1, 0), Z(3), W(2, 0), W(3, 0), W(0, 1), W(1, 1), W(2, 1), W(3, 1)]
-        products = (0, 0, 1, 1, 1, 0, 1, 1, 3, 3, 3, 2)
+        pairs = [Z(0), W(0, 0), Z(1), W(1, 0), Z(2), Z(3), W(2, 0), W(3, 0), W(0, 1), W(1, 1), W(2, 1), W(3, 1)]
+        products = (0, 0, 0, 0, 0, 0, 1, 1, 3, 3, 3, 2)
         M = [("M",)]
-        behind = M * 4 + R(0) + R(1)
+        behind = R(0) + R(1)
         given = 0
         for pair, n in zip(pairs, products):
             behind = behind + pair + dws[given:given + n] + M * (2 - n)
             given += n
         behind = behind + dws[given:]
-        on_vector = [("Z", 2, 1), ("Z", 3, 1)] + [("W", u, 1, 1) for u in range(4)]
-        pace = {"rope": 3, "h": 0, "qz": 1, "qh": 1, "qt": 1, "qw": 1, "s1": 1, "s2": 1, "s3": 1, "dh": 0}
+        on_vector = [("W", u, 1, 1) for u in range(4)] + [("D", 3, 6), ("D", 3, 7)]
+        pace = {"rope": 4, "h": 0, "qz": 1, "qh": 1, "qt": 1, "qw": 1, "s1": 1, "s2": 1, "s3": 1, "dh": 0}
         look = 2
         pos_pe = [0]
         pos_s = [0]

@@ -15,324 +15,288 @@ ALU = mybir.AluOpType
 ACT = mybir.ActivationFunctionType
 
 P = 128
-B, L, E, NH, HD = 4, 128, 1024, 8, 128
+B, L, E, HEADS, HD = 4, 128, 1024, 8, 128
 T = B * L
-J = NH * HD
+J = HEADS * HD
+SLOTS = 4
 UNIT = 512
 HALF = 512
+UNITS = 2 * J // UNIT
 FLOPS = 2 * 2 * T * E * 2 * J
 
-
-def R(h):
-    return [("R", h, j) for j in range(4)]
-
-
-def Z(u):
-    return [("Z", u, 0), ("Z", u, 1)]
-
-
-def W(u, h):
-    return [("W", u, h, 0), ("W", u, h, 1)]
+ORDER = """
+rope0 rg03 rg13
+rope1 rg12 rg02 dk2 dk3
+qz0 rg11 rg00
+qz1 tz01 rg01 tw101 cz01
+norm0 tz00 cw101 tw001 cz00
+qt0 tw000 cw001 tz11 cw000
+rope2 tw200 cz11 cw200
+rope3 tz10 rg10 cz10
+qh0 tw100 tw201 cw100 tz21 cw201
+norm1 tw301 cz21
+qz2 tw210 cw301 tw110 cw210
+qh1 tz30 cw110 tw300 cz30
+qw20 tz20 cw300 dw10 cz20
+qw10 dw20 cd10 dw00 cd20
+qt1 tz31 cd00 tw310 cz31v
+qz3 dw04 cw310 dw14 cd04
+qw00 tw311 cd14 dw11 cw311
+qw30 cd11 tw111 tw211 cw111
+qt2 dw21 cw211 dw05 cd21
+qt3 tw010 cd05v dw15 cw010v dh10
+qw11 tw011 cd15 cw011
+qw31
+gain10 dw01 dh00
+qw21 cd01 dw30 cd30
+qw01 dw02 dw16 cd02v cd16 dh11
+gain00 dw34 dw35 cd34
+gain11 dw31 cd35 dh20
+dot1 cd31 dw24 cd24 dw06 dh01
+gain20 dw17 cd06
+out1 cd17 dw36 dw07 cd36 cd07 dh31
+gain01 dw25
+dot0 dw37 cd25 dw12 cd37 cd12 dh21
+gain31 dw32 cd32
+out0 dw26 cd26 dw33 cd33 dh30
+gain21
+dot2 dw13 dw22 cd13
+gain30 dw03 cd22
+out2 dw23 cd03 cd23 dw27 cd27
+dot3
+out3
+"""
 
 
 def tile_llamaselfattentionblock_pa_v_kernel(tc, x, g, wq, wk, rstd, grad_0, grad_1, out_0, out_1, out_2):
     nc = tc.nc
     grads = (grad_0, grad_1)
     weights = (wq, wk)
-    outs = (out_1, out_2)
+    weight_grads = (out_1, out_2)
+    x_rows = x.flatten_outer_dims().rearrange("(p j) e -> p j e", j=SLOTS)
+    out_rows = out_0.flatten_outer_dims().rearrange("(p j) (h e) -> p j h e", j=SLOTS, h=2)
+
     with ExitStack() as ctx:
         keep = ctx.enter_context(tc.tile_pool(name="keep", bufs=1))
-        stage = ctx.enter_context(tc.tile_pool(name="stage", bufs=3))
+        reused = ctx.enter_context(tc.tile_pool(name="reused", bufs=2))
         psum = ctx.enter_context(tc.psum_pool(name="psum", bufs=1))
 
         def kept(name, shape, dtype):
             return keep.tile(shape, dtype, name=name, align_bytes=64)
 
-        r4 = kept("r4", [P, 4], F32)
-        grow = kept("grow", [P, E], BF16)
-        ones = kept("ones", [P, P], BF16)
-        ident = kept("ident", [P, P], F32)
-        xs = kept("xs", [P, 4, E], BF16)
-        gr = [kept("gr%d" % a, [P, NH, 4, HD], BF16) for a in range(2)]
-        wt = [[kept("wt%d%d" % (a, h), [P, 4, J], BF16) for h in range(2)] for a in range(2)]
-
-        ctx.enter_context(tc.manual_schedule())
-
-        nc.vector.memset(grow[:], 0.0)
-        nc.gpsimd.memset(ones[:], 1.0)
-        nc.sync.dma_start(out=r4[:], in_=rstd.rearrange("b (q j) -> (b q) j", j=4))
-        nc.sync.dma_start(out=grow[0:1, :], in_=g.rearrange("(o e) -> o e", o=1))
-
-        def load(name):
-            if name[0] == "X":
-                h = int(name[1])
-                nc.sync.dma_start(
-                    out=xs[:, :, h * HALF:(h + 1) * HALF],
-                    in_=x.flatten_outer_dims().rearrange("(p j) e -> p j e", j=4)[:, :, h * HALF:(h + 1) * HALF])
-            if name[0] == "W":
-                a, h = int(name[1]), int(name[2])
-                nc.sync.dma_start(
-                    out=wt[a][h][:],
-                    in_=weights[a][h * HALF:(h + 1) * HALF, :].rearrange("(p i) f -> p i f", i=4))
-
-        def load_grad(a, b, n0, n1):
-            queue = nc.sync if b < 2 else nc.scalar
-            queue.dma_start(out=gr[a][32 * b:32 * b + 32, n0:n1].rearrange("q n j d -> q n (j d)"),
-                            in_=grads[a][b, n0:n1].rearrange("n (q j) d -> q n (j d)", j=4))
-
-        for n0 in (0, 4):
-            for b in (0, 2, 1, 3):
-                load_grad(0, b, n0, n0 + 4)
-        load("X0")
-        load_grad(1, 0, 0, 8)
-        load_grad(1, 1, 0, 8)
-        for name in ("W00", "X1", "W10", "W01", "W11"):
-            load(name)
-
-        ints = kept("ints", [P, 4], I32)
-        pos = kept("pos", [P, 4], I32)
-        lt = kept("lt", [P, 4], F32)
-        coarse = kept("coarse", [P, 8], F32)
-        fine = kept("fine", [P, 8], F32)
-        theta = kept("theta", [P, 8, 8], F32)
-        turns = kept("turns", [P, 4, 64], F32)
-        whole = kept("whole", [P, 4, 64], I32)
-        part = kept("part", [P, 4, 64], F32)
-        cosines = kept("cosines", [P, 4, HD], F32)
-        nc.gpsimd.iota(ints[:], pattern=[[1, 4]], base=0, channel_multiplier=4)
-        make_identity(nc, ident[:])
-        nc.vector.memset(coarse[:], 1.0)
-        nc.vector.memset(fine[:], 1.0)
-        for s in (1, 2, 4):
-            nc.vector.tensor_single_scalar(coarse[:, s:2 * s], coarse[:, 0:s], 10000.0 ** (-s / 8.0), ALU.mult)
-            nc.vector.tensor_single_scalar(fine[:, s:2 * s], fine[:, 0:s], 10000.0 ** (-s / 64.0), ALU.mult)
-        nc.vector.tensor_single_scalar(pos[:], ints[:], L - 1, ALU.bitwise_and)
-        nc.vector.tensor_tensor(theta[:], coarse[:].unsqueeze(2).to_broadcast([P, 8, 8]),
-                                fine[:].unsqueeze(1).to_broadcast([P, 8, 8]), ALU.mult)
-        nc.vector.tensor_single_scalar(lt[:], pos[:], 0.5 / math.pi, ALU.mult)
-        nc.vector.tensor_tensor(turns[:], theta[:].rearrange("p a b -> p (a b)").unsqueeze(1).to_broadcast([P, 4, 64]),
-                                lt[:].unsqueeze(2).to_broadcast([P, 4, 64]), ALU.mult)
-        nc.vector.tensor_single_scalar(whole[:], turns[:], 0.25, ALU.add)
-        nc.vector.scalar_tensor_tensor(part[:].rearrange("p j i -> p (j i)"), turns[:].rearrange("p j i -> p (j i)"), 0.25,
-                                       whole[:].rearrange("p j i -> p (j i)"), ALU.add, ALU.subtract)
-        nc.scalar.activation(out=cosines[:].rearrange("p j (i s) -> p (j i) s", s=2),
-                             in_=part[:].rearrange("p j i -> p (j i)").unsqueeze(2).to_broadcast([P, 256, 2]),
-                             func=ACT.Sin, scale=2.0 * math.pi)
-        nr2 = kept("nr2", [P, 4], F32)
-        nc.vector.scalar_tensor_tensor(nr2[:], r4[:], -1.0 / E, r4[:], ALU.mult, ALU.mult)
-
-        rg = kept("rg", [P, 4, E], F32)
-        gps = []
-        for h in range(2):
-            bank = psum.tile([P, HALF], F32, name="gps%d" % h, tag="tr", bufs=3)
-            nc.tensor.matmul(bank[:], lhsT=ones[:], rhs=grow[:, h * HALF:(h + 1) * HALF], start=True, stop=True)
-            gps.append(bank)
-        warm = psum.tile([P, HALF], F32, name="warm", tag="dh", bufs=2)
-        load_grad(1, 2, 0, 8)
-
-        dz = [kept("dz%d" % u, [P, UNIT, 4], BF16) for u in range(4)]
-        zt = [kept("zt%d" % u, [P, 4, P, 4], BF16) for u in range(4)]
-        ht = [kept("ht%d" % h, [P, HALF, 4], BF16) for h in range(2)]
-        wg = {}
-
         def codes(name):
             return kept(name + "_codes", [P, 512], U32), kept(name + "_scales", [P, 512], U8)
 
-        dzq = [codes("dzq%d" % u) for u in range(4)]
-        ztq = [codes("ztq%d" % u) for u in range(4)]
-        htq = [codes("htq%d" % h) for h in range(2)]
-        wgq = [[codes("wgq%d%d" % (u, h)) for h in range(2)] for u in range(4)]
-        ra = [kept("ra%d" % j, [P, E], F32) for j in range(4)]
-        coef = [kept("coef%d" % j, [P, 1], F32) for j in range(4)]
+        grad_sb = [reused.tile([P, HEADS, SLOTS, HD], BF16, name="grad%d" % a, tag="early_late", bufs=2, align_bytes=64) for a in range(2)]
+        pairs = [reused.tile([P, 2, 2, HALF], F32, name="pair%d" % i, tag="early_late", bufs=2, align_bytes=64) for i in range(2)]
+        scaled = [pairs[j // 2][:, j % 2] for j in range(SLOTS)]
+        rstd_sb = kept("rstd_sb", [P, SLOTS], F32)
+        gain_row = kept("gain_row", [P, E], BF16)
+        ones = kept("ones", [P, P], BF16)
+        identity = kept("identity", [P, P], F32)
+        x_sb = kept("x_sb", [P, 2, SLOTS, HALF], BF16)
+        rg = kept("rg", [P, 2, SLOTS, HALF], F32)
+        w_sb = [[kept("w%d%d" % (a, h), [P, 4, J], BF16) for h in range(2)] for a in range(2)]
+        h_tok = [kept("h_tok%d" % h, [P, HALF, SLOTS], BF16) for h in range(2)]
+        dz_tok = [kept("dz_tok%d" % u, [P, UNIT, SLOTS], BF16) for u in range(UNITS)]
+        dz_feat = [kept("dz_feat%d" % u, [P, SLOTS, P, 4], BF16) for u in range(UNITS)]
+        w_feat = [[kept("w_feat%d%d" % (u, h), [P, HALF, 4], BF16) for h in range(2)] for u in range(UNITS)]
+        h_q = [codes("h_q%d" % h) for h in range(2)]
+        dz_tok_q = [codes("dz_tok_q%d" % u) for u in range(UNITS)]
+        dz_feat_q = [codes("dz_feat_q%d" % u) for u in range(UNITS)]
+        w_q = [[codes("w_q%d%d" % (u, h)) for h in range(2)] for u in range(UNITS)]
+        neg_r2 = kept("neg_r2", [P, SLOTS], F32)
+        coef = [kept("coef%d" % j, [P, 1], F32) for j in range(SLOTS)]
+
+        ctx.enter_context(tc.manual_schedule())
+
+        def load_grad(a, b, n0, n1, queue):
+            queue.dma_start(out=grad_sb[a][32 * b : 32 * b + 32, n0:n1].rearrange("q n j d -> q n (j d)"),
+                            in_=grads[a][b, n0:n1].rearrange("n (q j) d -> q n (j d)", j=SLOTS))
+
+        def load_x(h):
+            nc.sync.dma_start(out=x_sb[:, h], in_=x_rows[:, :, h * HALF : (h + 1) * HALF])
+
+        def load_w(a, h):
+            nc.sync.dma_start(out=w_sb[a][h][:], in_=weights[a][h * HALF : (h + 1) * HALF, :].rearrange("(q i) f -> q i f", i=4))
+
+        tokens = kept("tokens", [P, SLOTS], I32)
+        nc.gpsimd.iota(tokens[:], pattern=[[1, SLOTS]], base=0, channel_multiplier=SLOTS)
+        make_identity(nc, identity[:])
+        nc.vector.memset(gain_row[:], 0.0)
+        nc.vector.memset(ones[:], 1.0)
+        nc.sync.dma_start(out=rstd_sb[:], in_=rstd.rearrange("b (q j) -> (b q) j", j=SLOTS))
+        load_grad(0, 0, 0, 4, nc.sync)
+        load_grad(0, 2, 0, 4, nc.scalar)
+        load_grad(0, 1, 0, 4, nc.sync)
+        nc.scalar.dma_start(out=gain_row[0:1, :], in_=g.rearrange("(o e) -> o e", o=1))
+        load_grad(0, 3, 0, 4, nc.scalar)
+        load_grad(0, 2, 4, 8, nc.scalar)
+        load_grad(0, 3, 4, 8, nc.scalar)
+        load_grad(0, 0, 4, 8, nc.sync)
+        load_grad(0, 1, 4, 8, nc.sync)
+        load_w(0, 0)
+        load_x(0)
+        load_w(1, 0)
+        load_grad(1, 0, 0, HEADS, nc.sync)
+        load_grad(1, 1, 0, HEADS, nc.sync)
+        load_w(1, 1)
+        load_w(0, 1)
+        load_x(1)
+
+        positions = kept("positions", [P, SLOTS], I32)
+        theta_hi = kept("theta_hi", [P, 8], F32)
+        theta_lo = kept("theta_lo", [P, 8], F32)
+        theta = kept("theta", [P, 8, 8], F32)
+        turn_unit = kept("turn_unit", [P, SLOTS], F32)
+        turns = kept("turns", [P, SLOTS, HD // 2], F32)
+        whole = kept("whole", [P, SLOTS, HD // 2], I32)
+        fraction = kept("fraction", [P, SLOTS, HD // 2], F32)
+        cosines = kept("cosines", [P, SLOTS, HD], F32)
+        nc.vector.memset(theta_hi[:], 1.0)
+        nc.vector.memset(theta_lo[:], 1.0)
+        for s in (1, 2, 4):
+            nc.vector.tensor_single_scalar(theta_hi[:, s : 2 * s], theta_hi[:, 0:s], 10000.0 ** (-s / 8.0), ALU.mult)
+            nc.vector.tensor_single_scalar(theta_lo[:, s : 2 * s], theta_lo[:, 0:s], 10000.0 ** (-s / 64.0), ALU.mult)
+        nc.vector.tensor_single_scalar(positions[:], tokens[:], L - 1, ALU.bitwise_and)
+        nc.vector.tensor_tensor(theta[:], theta_hi[:].unsqueeze(2).to_broadcast([P, 8, 8]),
+                                theta_lo[:].unsqueeze(1).to_broadcast([P, 8, 8]), ALU.mult)
+        nc.vector.tensor_single_scalar(turn_unit[:], positions[:], 0.5 / math.pi, ALU.mult)
+        nc.vector.tensor_tensor(turns[:], theta[:].rearrange("p a b -> p (a b)").unsqueeze(1).to_broadcast([P, SLOTS, HD // 2]),
+                                turn_unit[:].unsqueeze(2).to_broadcast([P, SLOTS, HD // 2]), ALU.mult)
+        nc.vector.tensor_single_scalar(whole[:], turns[:], 0.25, ALU.add)
+        nc.vector.scalar_tensor_tensor(fraction[:].rearrange("p j i -> p (j i)"), turns[:].rearrange("p j i -> p (j i)"), 0.25,
+                                       whole[:].rearrange("p j i -> p (j i)"), ALU.add, ALU.subtract)
+        nc.scalar.activation(out=cosines[:].rearrange("p j (i s) -> p (j i) s", s=2),
+                             in_=fraction[:].rearrange("p j i -> p (j i)").unsqueeze(2).to_broadcast([P, SLOTS * HD // 2, 2]),
+                             func=ACT.Sin, scale=2.0 * math.pi)
+        nc.vector.scalar_tensor_tensor(neg_r2[:], rstd_sb[:], -1.0 / E, rstd_sb[:], ALU.mult, ALU.mult)
+
+        gain = psum.tile([P, E], BF16, name="gain", tag="dh", bufs=2)
+        for h in range(2):
+            cols = slice(h * HALF, (h + 1) * HALF)
+            nc.tensor.matmul(gain[:, cols], lhsT=ones[:], rhs=gain_row[:, cols], start=True, stop=True)
+
+        banks = {}
+
+        def dk(b):
+            load_grad(1, b, 0, HEADS, nc.scalar)
+
+        def rg_step(h, j):
+            nc.scalar.activation(out=rg[:, h, j], in_=gain[:, h * HALF : (h + 1) * HALF], func=ACT.Copy, scale=rstd_sb[:, j : j + 1])
 
         def rope(u):
             for n in range(4):
                 nc.vector.tensor_tensor(
-                    out=dz[u][:, n * HD:(n + 1) * HD, :].rearrange("p (c i) j -> p c j i", i=4),
-                    in0=gr[u // 2][:, 4 * (u % 2) + n].rearrange("p j (c i) -> p c j i", i=4),
+                    out=dz_tok[u][:, n * HD : (n + 1) * HD, :].rearrange("p (c i) j -> p c j i", i=4),
+                    in0=grad_sb[u // 2][:, 4 * (u % 2) + n].rearrange("p j (c i) -> p c j i", i=4),
                     in1=cosines[:].rearrange("p j (c i) -> p c j i", i=4),
                     op=ALU.mult)
 
-        def quantize(pair, dtype, src):
-            nc.vector.quantize_mx(out=pair[0][:].bitcast(dtype), scales=pair[1][:], in_=src)
-
-        def normed(h):
+        def norm(h):
             for c in range(2):
-                cols = slice(h * HALF + 256 * c, h * HALF + 256 * (c + 1))
+                cols = slice(c * HALF // 2, (c + 1) * HALF // 2)
                 nc.vector.tensor_tensor(
-                    out=ht[h][:, 256 * c:256 * (c + 1), :].rearrange("p (c i) j -> p c j i", i=4),
-                    in0=xs[:, :, cols].rearrange("p j (c i) -> p c j i", i=4),
-                    in1=rg[:, :, cols].rearrange("p j (c i) -> p c j i", i=4), op=ALU.mult)
+                    out=h_tok[h][:, cols, :].rearrange("p (c i) j -> p c j i", i=4),
+                    in0=x_sb[:, h, :, cols].rearrange("p j (c i) -> p c j i", i=4),
+                    in1=rg[:, h, :, cols].rearrange("p j (c i) -> p c j i", i=4),
+                    op=ALU.mult)
 
-        banks = {}
+        def quantize(pair, dtype, values):
+            nc.vector.quantize_mx(out=pair[0][:].bitcast(dtype), scales=pair[1][:], in_=values)
 
-        def pe(b):
-            k = b[0]
-            if k == "M":
-                nc.tensor.matmul(warm[:], lhsT=ones[:], rhs=grow[:, 0:HALF], start=True, stop=True)
-                return
-            if k == "Z":
-                u, jp = b[1:]
-                bank = psum.tile([P, 4, P], F32, name="tr", tag="tr", bufs=3)
-                words = dz[u][:].rearrange("p c j -> p (c j)").bitcast(F32)
-                for t in range(4):
-                    nc.tensor.transpose(bank[:, t, :], words[:, 2 * t + jp:2 * UNIT:8], ident[:])
-            elif k == "W":
-                u, h, ip = b[1:]
-                bank = psum.tile([P, 4, P], F32, name="tr", tag="tr", bufs=3)
-                words = wt[u // 2][h][:].rearrange("p i f -> p (i f)").bitcast(F32)
-                for i2 in range(2):
-                    for ul in range(2):
-                        w0 = (2 * ip + i2) * (J // 2) + (u % 2) * (UNIT // 2)
-                        nc.tensor.transpose(bank[:, 2 * i2 + ul, :], words[:, w0 + ul:w0 + UNIT // 2:2], ident[:])
-            else:
-                u, e = b[1:]
-                bank = psum.tile([P, UNIT], F32, name="dw", tag="dw", bufs=3)
-                hc, hs = htq[e // 4]
-                cols = slice((e % 4) * P, (e % 4 + 1) * P)
-                nc.tensor.matmul_mx(out=bank[:], lhsT=hc[:, cols].bitcast(E4M3), lhsT_scale=hs[:, cols],
-                                    rhs=dzq[u][0][:].bitcast(E5M2), rhs_scale=dzq[u][1][:], start=True, stop=True)
-            banks[b] = bank
+        def qz(u):
+            quantize(dz_tok_q[u], E5M2, dz_tok[u][:].rearrange("p c j -> p (c j)"))
 
-        def copy(engine, out, in_):
-            if engine == "V":
+        def qh(h):
+            quantize(h_q[h], E4M3, h_tok[h][:].rearrange("p c j -> p (c j)"))
+
+        def qt(u):
+            quantize(dz_feat_q[u], E5M2, dz_feat[u][:].rearrange("p j q t -> p (j q t)"))
+
+        def qw(u, h):
+            quantize(w_q[u][h], E4M3, w_feat[u][h][:].rearrange("p c t -> p (c t)"))
+
+        def tz(u, jp):
+            bank = psum.tile([P, 4, P], F32, name="tr", tag="tr", bufs=3)
+            words = dz_tok[u][:].rearrange("p c j -> p (c j)").bitcast(F32)
+            for t in range(4):
+                nc.tensor.transpose(bank[:, t, :], words[:, 2 * t + jp : 2 * UNIT : 8], identity[:])
+            banks["z", u, jp] = bank
+
+        def tw(u, h, ip):
+            bank = psum.tile([P, 4, P], F32, name="tr", tag="tr", bufs=3)
+            words = w_sb[u // 2][h][:].rearrange("p i f -> p (i f)").bitcast(F32)
+            for i in range(2):
+                first = (2 * ip + i) * (J // 2) + (u % 2) * (UNIT // 2)
+                for s in range(2):
+                    nc.tensor.transpose(bank[:, 2 * i + s, :], words[:, first + s : first + UNIT // 2 : 2], identity[:])
+            banks["w", u, h, ip] = bank
+
+        def dw(u, e):
+            bank = psum.tile([P, UNIT], F32, name="dw", tag="dw", bufs=3)
+            lhs, lhs_scale = h_q[e // 4]
+            rhs, rhs_scale = dz_tok_q[u]
+            cols = slice((e % 4) * P, (e % 4 + 1) * P)
+            nc.tensor.matmul_mx(out=bank[:], lhsT=lhs[:, cols].bitcast(E4M3), lhsT_scale=lhs_scale[:, cols],
+                                rhs=rhs[:].bitcast(E5M2), rhs_scale=rhs_scale[:], start=True, stop=True)
+            banks["d", u, e] = bank
+
+        def copy(on_vector, out, in_):
+            if on_vector:
                 nc.vector.tensor_copy(out=out, in_=in_)
             else:
                 nc.scalar.copy(out=out, in_=in_)
 
-        def drain(b, engine):
-            k = b[0]
-            if k == "M":
-                return
-            if k == "R":
-                h, j = b[1:]
-                nc.scalar.activation(out=rg[:, j, h * HALF:(h + 1) * HALF], in_=gps[h][:], func=ACT.Copy, scale=r4[:, j:j + 1])
-                if (h, j) == (0, 0):
-                    load_grad(1, 3, 0, 8)
-                return
-            bank = banks.pop(b)
-            if k == "Z":
-                u, jp = b[1:]
-                copy(engine, zt[u][:, 2 * jp:2 * jp + 2],
-                     bank[:].rearrange("p t q -> p (t q)").bitcast(BF16).rearrange("p (t q e) -> p e q t", t=4, e=2))
-            elif k == "W":
-                u, h, ip = b[1:]
-                if (u, h) not in wg:
-                    wg[(u, h)] = stage.tile([P, HALF, 4], BF16, name="wg", tag="wg", bufs=4, align_bytes=64)
-                dst = wg[(u, h)][:].rearrange("p c t -> p (c t)").bitcast(F32).rearrange("p (q w) -> p q w", w=8)
-                copy(engine, dst[:, :, 4 * ip:4 * ip + 4], bank[:].rearrange("p c q -> p q c"))
-            else:
-                u, e = b[1:]
-                st = stage.tile([P, UNIT], F32, name="st", tag="st", bufs=8)
-                copy(engine, st[:], bank[:])
-                nc.sync.dma_start(out=outs[u // 2][e * P:(e + 1) * P, (u % 2) * UNIT:(u % 2 + 1) * UNIT], in_=st[:])
+        def cz(on_vector, u, jp):
+            bank = banks["z", u, jp]
+            copy(on_vector, dz_feat[u][:, 2 * jp : 2 * jp + 2],
+                 bank[:].rearrange("p t q -> p (t q)").bitcast(BF16).rearrange("p (t q s) -> p s q t", t=4, s=2))
 
-        dhb = {}
+        def cw(on_vector, u, h, ip):
+            bank = banks["w", u, h, ip]
+            rows = w_feat[u][h][:].rearrange("p c t -> p (c t)").bitcast(F32).rearrange("p (q w) -> p q w", w=8)
+            copy(on_vector, rows[:, :, 4 * ip : 4 * ip + 4], bank[:].rearrange("p w q -> p q w"))
+
+        def cd(on_vector, u, e):
+            tile = reused.tile([P, UNIT], F32, name="store", tag="store", bufs=8)
+            copy(on_vector, tile[:], banks["d", u, e][:])
+            nc.sync.dma_start(out=weight_grads[u // 2][e * P : (e + 1) * P, (u % 2) * UNIT : (u % 2 + 1) * UNIT], in_=tile[:])
 
         def dh(j, h):
             bank = psum.tile([P, HALF], F32, name="dh", tag="dh", bufs=2)
             cols = slice(j * P, (j + 1) * P)
-            for u in range(4):
-                nc.tensor.matmul_mx(out=bank[:], lhsT=ztq[u][0][:, cols].bitcast(E5M2), lhsT_scale=ztq[u][1][:, cols],
-                                    rhs=wgq[u][h][0][:].bitcast(E4M3), rhs_scale=wgq[u][h][1][:],
-                                    start=(u == 0), stop=(u == 3))
-            dhb[(j, h)] = bank
+            for u in range(UNITS):
+                lhs, lhs_scale = dz_feat_q[u]
+                rhs, rhs_scale = w_q[u][h]
+                nc.tensor.matmul_mx(out=bank[:], lhsT=lhs[:, cols].bitcast(E5M2), lhsT_scale=lhs_scale[:, cols],
+                                    rhs=rhs[:].bitcast(E4M3), rhs_scale=rhs_scale[:], start=(u == 0), stop=(u == UNITS - 1))
+            banks["h", j, h] = bank
 
-        def s1(j, h):
-            cols = slice(h * HALF, (h + 1) * HALF)
-            nc.vector.tensor_tensor(out=ra[j][:, cols], in0=dhb[(j, h)][:], in1=rg[:, j, cols], op=ALU.mult)
+        def scale(j, h):
+            nc.vector.tensor_tensor(out=scaled[j][:, h], in0=banks["h", j, h][:], in1=rg[:, h, j], op=ALU.mult)
 
-        def s2(j):
-            junk = stage.tile([P, E], F32, name="junk", tag="junk", bufs=2)
-            nc.vector.scalar_tensor_tensor(junk[:], xs[:, j, :], nr2[:, j:j + 1], ra[j][:], ALU.mult, ALU.mult, accum_out=coef[j][:])
+        def dot(j):
+            product = reused.tile([P, 2, HALF], F32, name="product", tag="product", bufs=2)
+            nc.vector.scalar_tensor_tensor(product[:], x_sb[:, :, j], neg_r2[:, j : j + 1], scaled[j], ALU.mult, ALU.mult,
+                                           accum_out=coef[j][:])
 
-        def s3(j):
-            res = stage.tile([P, E], F32, name="res", tag="res", bufs=2)
-            nc.vector.scalar_tensor_tensor(res[:], xs[:, j, :], coef[j][:], ra[j][:], ALU.mult, ALU.add)
-            nc.sync.dma_start(out=out_0.flatten_outer_dims().rearrange("(p j) e -> p j e", j=4)[:, j, :], in_=res[:])
+        def out(j, pieces):
+            result = reused.tile([P, 2, HALF], F32, name="result", tag="result", bufs=2)
+            for piece in pieces:
+                nc.vector.scalar_tensor_tensor(result[:, piece], x_sb[:, piece, j], coef[j][:], scaled[j][:, piece], ALU.mult, ALU.add)
+                nc.sync.dma_start(out=out_rows[:, j, piece], in_=result[:, piece])
 
-        vector = [("rope", 0), ("rope", 1), ("rope", 2), ("rope", 3), ("h", 0), ("qz", 0), ("h", 1), ("qh", 0), ("qz", 1), ("qt", 0), ("qz", 2),
-                  ("qh", 1), ("qw", 0, 0), ("qt", 1), ("qz", 3), ("qw", 1, 0), ("qt", 2), ("qw", 2, 0), ("qt", 3), ("qw", 3, 0),
-                  ("qw", 0, 1), ("qw", 1, 1), ("qw", 2, 1), ("qw", 3, 1),
-                  ("dh", 0, 0), ("dh", 0, 1), ("s1", 0, 0), ("s1", 0, 1), ("dh", 1, 0), ("dh", 1, 1), ("s1", 1, 0), ("s2", 0), ("s1", 1, 1),
-                  ("dh", 2, 0), ("dh", 2, 1), ("s3", 0), ("s1", 2, 0), ("s2", 1), ("s1", 2, 1), ("dh", 3, 0), ("dh", 3, 1), ("s3", 1),
-                  ("s1", 3, 0), ("s2", 2), ("s1", 3, 1), ("s3", 2), ("s2", 3), ("s3", 3)]
-        dws = [("D", u, e) for u in range(4) for e in range(8)]
-        pairs = [Z(0), W(0, 0), Z(1), W(1, 0), Z(2), Z(3), W(2, 0), W(3, 0), W(0, 1), W(1, 1), W(2, 1), W(3, 1)]
-        products = (0, 0, 0, 0, 0, 0, 1, 1, 3, 3, 3, 2)
-        M = [("M",)]
-        behind = R(0) + R(1)
-        given = 0
-        for pair, n in zip(pairs, products):
-            behind = behind + pair + dws[given:given + n] + M * (2 - n)
-            given += n
-        behind = behind + dws[given:]
-        on_vector = [("W", u, 1, 1) for u in range(4)] + [("D", 3, 6), ("D", 3, 7)]
-        pace = {"rope": 4, "h": 0, "qz": 1, "qh": 1, "qt": 1, "qw": 1, "s1": 1, "s2": 1, "s3": 1, "dh": 0}
-        look = 2
-        pos_pe = [0]
-        pos_s = [0]
-        made = set()
-
-        def can_pe(b):
-            if b[0] in ("R", "M"):
-                return True
-            waiting = [c for c in behind[pos_s[0]:pos_pe[0]] if c[0] not in ("R", "M") and (c[0] == "D") == (b[0] == "D")]
-            if len(waiting) >= 3:
-                return False
-            if b[0] == "Z":
-                return ("rope", b[1]) in made
-            if b[0] == "D":
-                return ("qz", b[1]) in made and ("qh", b[2] // 4) in made
-            return True
-
-        def pump(n):
-            for i in range(n):
-                if pos_s[0] >= len(behind):
-                    return
-                while pos_pe[0] < min(len(behind), pos_s[0] + 1 + look) and can_pe(behind[pos_pe[0]]):
-                    if behind[pos_pe[0]][0] != "R":
-                        pe(behind[pos_pe[0]])
-                    pos_pe[0] += 1
-                if pos_pe[0] <= pos_s[0]:
-                    return
-                drain(behind[pos_s[0]], "V" if behind[pos_s[0]] in on_vector else "S")
-                pos_s[0] += 1
-                while pos_s[0] < pos_pe[0] and behind[pos_s[0]][0] == "M":
-                    pos_s[0] += 1
-
-        def need(kind, *key):
-            while any(b[0] == kind and b[1:1 + len(key)] == key for b in behind[pos_s[0]:]):
-                before = pos_s[0]
-                pump(1)
-                assert pos_s[0] > before, "stuck"
-
-        for v in vector:
-            k = v[0]
-            if k == "rope":
-                rope(v[1])
-            elif k == "h":
-                need("R", v[1])
-                normed(v[1])
-            elif k == "qz":
-                quantize(dzq[v[1]], E5M2, dz[v[1]][:].rearrange("p c j -> p (c j)"))
-            elif k == "qh":
-                quantize(htq[v[1]], E4M3, ht[v[1]][:].rearrange("p c j -> p (c j)"))
-            elif k == "qt":
-                need("Z", v[1])
-                quantize(ztq[v[1]], E5M2, zt[v[1]][:].rearrange("p j q t -> p (j q t)"))
-            elif k == "qw":
-                need("W", v[1], v[2])
-                quantize(wgq[v[1]][v[2]], E4M3, wg[(v[1], v[2])][:].rearrange("p c t -> p (c t)"))
-            elif k == "dh":
-                dh(v[1], v[2])
-            elif k == "s1":
-                s1(v[1], v[2])
-            elif k == "s2":
-                s2(v[1])
+        steps = {"dk": dk, "rope": rope, "norm": norm, "qz": qz, "qh": qh, "qt": qt, "qw": qw, "tz": tz, "tw": tw, "dw": dw,
+                 "dh": dh, "rg": rg_step, "gain": scale, "dot": dot}
+        copies = {"cz": cz, "cw": cw, "cd": cd}
+        order = ORDER.split()
+        for step in order:
+            digits = [int(c) for c in step if c in "0123456789"]
+            kind = [k for k in list(steps) + list(copies) + ["out"] if step.startswith(k)][0]
+            if kind in copies:
+                copies[kind](step[-1] == "v", *digits)
+            elif kind == "out":
+                out(digits[0], [slice(0, 1), slice(1, 2)] if step == order[-1] else [slice(0, 2)])
             else:
-                s3(v[1])
-            made.add(v)
-            pump(pace[k])
-        while pos_s[0] < len(behind):
-            pump(1)
+                steps[kind](*digits)

import math
from contextlib import ExitStack

import concourse.mybir as mybir
from concourse.masks import make_identity

F32 = mybir.dt.float32
BF16 = mybir.dt.bfloat16
I32 = mybir.dt.int32
U32 = mybir.dt.uint32
U8 = mybir.dt.uint8
E4M3 = mybir.dt.float8_e4m3fn_x4
E5M2 = mybir.dt.float8_e5m2_x4
ALU = mybir.AluOpType
ACT = mybir.ActivationFunctionType

P = 128
B, L, E, HEADS, HD = 4, 128, 1024, 8, 128
T = B * L
J = HEADS * HD
SLOTS = 4
UNIT = 512
HALF = 512
UNITS = 2 * J // UNIT
FLOPS = 2 * 2 * T * E * 2 * J

ORDER = """
rope0 rg03 rg13
rope1 rg12 rg02 dk2 dk3
qz0 rg11 rg00
qz1 tz01 rg01 tw101 cz01
norm0 tz00 cw101 tw001 cz00
qt0 tw000 cw001 tz11 cw000
rope2 tw200 cz11 cw200
rope3 tz10 rg10 cz10
qh0 tw100 tw201 cw100 tz21 cw201
norm1 tw301 cz21
qz2 tw210 cw301 tw110 cw210
qh1 tz30 cw110 tw300 cz30
qw20 tz20 cw300 dw10 cz20
qw10 dw20 cd10 dw00 cd20
qt1 tz31 cd00 tw310 cz31v
qz3 dw04 cw310 dw14 cd04
qw00 tw311 cd14 dw11 cw311
qw30 cd11 tw111 tw211 cw111
qt2 dw21 cw211 dw05 cd21
qt3 tw010 cd05v dw15 cw010v dh10
qw11 tw011 cd15 cw011
qw31
gain10 dw01 dh00
qw21 cd01 dw30 cd30
qw01 dw02 dw16 cd02v cd16 dh11
gain00 dw34 dw35 cd34
gain11 dw31 cd35 dh20
dot1 cd31 dw24 cd24 dw06 dh01
gain20 dw17 cd06
out1 cd17 dw36 dw07 cd36 cd07 dh31
gain01 dw25
dot0 dw37 cd25 dw12 cd37 cd12 dh21
gain31 dw32 cd32
out0 dw26 cd26 dw33 cd33 dh30
gain21
dot2 dw13 dw22 cd13
gain30 dw03 cd22
out2 dw23 cd03 cd23 dw27 cd27
dot3
out3
"""


def tile_llamaselfattentionblock_pa_v_kernel(tc, x, g, wq, wk, rstd, grad_0, grad_1, out_0, out_1, out_2):
    nc = tc.nc
    grads = (grad_0, grad_1)
    weights = (wq, wk)
    weight_grads = (out_1, out_2)
    x_rows = x.flatten_outer_dims().rearrange("(p j) e -> p j e", j=SLOTS)
    out_rows = out_0.flatten_outer_dims().rearrange("(p j) (h e) -> p j h e", j=SLOTS, h=2)

    with ExitStack() as ctx:
        keep = ctx.enter_context(tc.tile_pool(name="keep", bufs=1))
        reused = ctx.enter_context(tc.tile_pool(name="reused", bufs=2))
        psum = ctx.enter_context(tc.psum_pool(name="psum", bufs=1))

        def kept(name, shape, dtype):
            return keep.tile(shape, dtype, name=name, align_bytes=64)

        def codes(name):
            return kept(name + "_codes", [P, 512], U32), kept(name + "_scales", [P, 512], U8)

        grad_sb = [reused.tile([P, HEADS, SLOTS, HD], BF16, name="grad%d" % a, tag="early_late", bufs=2, align_bytes=64) for a in range(2)]
        pairs = [reused.tile([P, 2, 2, HALF], F32, name="pair%d" % i, tag="early_late", bufs=2, align_bytes=64) for i in range(2)]
        scaled = [pairs[j // 2][:, j % 2] for j in range(SLOTS)]
        rstd_sb = kept("rstd_sb", [P, SLOTS], F32)
        gain_row = kept("gain_row", [P, E], BF16)
        ones = kept("ones", [P, P], BF16)
        identity = kept("identity", [P, P], F32)
        x_sb = kept("x_sb", [P, 2, SLOTS, HALF], BF16)
        rg = kept("rg", [P, 2, SLOTS, HALF], F32)
        w_sb = [[kept("w%d%d" % (a, h), [P, 4, J], BF16) for h in range(2)] for a in range(2)]
        h_tok = [kept("h_tok%d" % h, [P, HALF, SLOTS], BF16) for h in range(2)]
        dz_tok = [kept("dz_tok%d" % u, [P, UNIT, SLOTS], BF16) for u in range(UNITS)]
        dz_feat = [kept("dz_feat%d" % u, [P, SLOTS, P, 4], BF16) for u in range(UNITS)]
        w_feat = [[kept("w_feat%d%d" % (u, h), [P, HALF, 4], BF16) for h in range(2)] for u in range(UNITS)]
        h_q = [codes("h_q%d" % h) for h in range(2)]
        dz_tok_q = [codes("dz_tok_q%d" % u) for u in range(UNITS)]
        dz_feat_q = [codes("dz_feat_q%d" % u) for u in range(UNITS)]
        w_q = [[codes("w_q%d%d" % (u, h)) for h in range(2)] for u in range(UNITS)]
        neg_r2 = kept("neg_r2", [P, SLOTS], F32)
        coef = [kept("coef%d" % j, [P, 1], F32) for j in range(SLOTS)]

        ctx.enter_context(tc.manual_schedule())

        def load_grad(a, b, n0, n1, queue):
            queue.dma_start(out=grad_sb[a][32 * b : 32 * b + 32, n0:n1].rearrange("q n j d -> q n (j d)"),
                            in_=grads[a][b, n0:n1].rearrange("n (q j) d -> q n (j d)", j=SLOTS))

        def load_x(h):
            nc.sync.dma_start(out=x_sb[:, h], in_=x_rows[:, :, h * HALF : (h + 1) * HALF])

        def load_w(a, h):
            nc.sync.dma_start(out=w_sb[a][h][:], in_=weights[a][h * HALF : (h + 1) * HALF, :].rearrange("(q i) f -> q i f", i=4))

        tokens = kept("tokens", [P, SLOTS], I32)
        nc.gpsimd.iota(tokens[:], pattern=[[1, SLOTS]], base=0, channel_multiplier=SLOTS)
        make_identity(nc, identity[:])
        nc.vector.memset(gain_row[:], 0.0)
        nc.vector.memset(ones[:], 1.0)
        nc.sync.dma_start(out=rstd_sb[:], in_=rstd.rearrange("b (q j) -> (b q) j", j=SLOTS))
        load_grad(0, 0, 0, 4, nc.sync)
        load_grad(0, 2, 0, 4, nc.scalar)
        load_grad(0, 1, 0, 4, nc.sync)
        nc.scalar.dma_start(out=gain_row[0:1, :], in_=g.rearrange("(o e) -> o e", o=1))
        load_grad(0, 3, 0, 4, nc.scalar)
        load_grad(0, 2, 4, 8, nc.scalar)
        load_grad(0, 3, 4, 8, nc.scalar)
        load_grad(0, 0, 4, 8, nc.sync)
        load_grad(0, 1, 4, 8, nc.sync)
        load_w(0, 0)
        load_x(0)
        load_w(1, 0)
        load_grad(1, 0, 0, HEADS, nc.sync)
        load_grad(1, 1, 0, HEADS, nc.sync)
        load_w(1, 1)
        load_w(0, 1)
        load_x(1)

        positions = kept("positions", [P, SLOTS], I32)
        theta_hi = kept("theta_hi", [P, 8], F32)
        theta_lo = kept("theta_lo", [P, 8], F32)
        theta = kept("theta", [P, 8, 8], F32)
        turn_unit = kept("turn_unit", [P, SLOTS], F32)
        turns = kept("turns", [P, SLOTS, HD // 2], F32)
        whole = kept("whole", [P, SLOTS, HD // 2], I32)
        fraction = kept("fraction", [P, SLOTS, HD // 2], F32)
        cosines = kept("cosines", [P, SLOTS, HD], F32)
        nc.vector.memset(theta_hi[:], 1.0)
        nc.vector.memset(theta_lo[:], 1.0)
        for s in (1, 2, 4):
            nc.vector.tensor_single_scalar(theta_hi[:, s : 2 * s], theta_hi[:, 0:s], 10000.0 ** (-s / 8.0), ALU.mult)
            nc.vector.tensor_single_scalar(theta_lo[:, s : 2 * s], theta_lo[:, 0:s], 10000.0 ** (-s / 64.0), ALU.mult)
        nc.vector.tensor_single_scalar(positions[:], tokens[:], L - 1, ALU.bitwise_and)
        nc.vector.tensor_tensor(theta[:], theta_hi[:].unsqueeze(2).to_broadcast([P, 8, 8]),
                                theta_lo[:].unsqueeze(1).to_broadcast([P, 8, 8]), ALU.mult)
        nc.vector.tensor_single_scalar(turn_unit[:], positions[:], 0.5 / math.pi, ALU.mult)
        nc.vector.tensor_tensor(turns[:], theta[:].rearrange("p a b -> p (a b)").unsqueeze(1).to_broadcast([P, SLOTS, HD // 2]),
                                turn_unit[:].unsqueeze(2).to_broadcast([P, SLOTS, HD // 2]), ALU.mult)
        nc.vector.tensor_single_scalar(whole[:], turns[:], 0.25, ALU.add)
        nc.vector.scalar_tensor_tensor(fraction[:].rearrange("p j i -> p (j i)"), turns[:].rearrange("p j i -> p (j i)"), 0.25,
                                       whole[:].rearrange("p j i -> p (j i)"), ALU.add, ALU.subtract)
        nc.scalar.activation(out=cosines[:].rearrange("p j (i s) -> p (j i) s", s=2),
                             in_=fraction[:].rearrange("p j i -> p (j i)").unsqueeze(2).to_broadcast([P, SLOTS * HD // 2, 2]),
                             func=ACT.Sin, scale=2.0 * math.pi)
        nc.vector.scalar_tensor_tensor(neg_r2[:], rstd_sb[:], -1.0 / E, rstd_sb[:], ALU.mult, ALU.mult)

        gain = psum.tile([P, E], BF16, name="gain", tag="dh", bufs=2)
        for h in range(2):
            cols = slice(h * HALF, (h + 1) * HALF)
            nc.tensor.matmul(gain[:, cols], lhsT=ones[:], rhs=gain_row[:, cols], start=True, stop=True)

        banks = {}

        def dk(b):
            load_grad(1, b, 0, HEADS, nc.scalar)

        def rg_step(h, j):
            nc.scalar.activation(out=rg[:, h, j], in_=gain[:, h * HALF : (h + 1) * HALF], func=ACT.Copy, scale=rstd_sb[:, j : j + 1])

        def rope(u):
            for n in range(4):
                nc.vector.tensor_tensor(
                    out=dz_tok[u][:, n * HD : (n + 1) * HD, :].rearrange("p (c i) j -> p c j i", i=4),
                    in0=grad_sb[u // 2][:, 4 * (u % 2) + n].rearrange("p j (c i) -> p c j i", i=4),
                    in1=cosines[:].rearrange("p j (c i) -> p c j i", i=4),
                    op=ALU.mult)

        def norm(h):
            for c in range(2):
                cols = slice(c * HALF // 2, (c + 1) * HALF // 2)
                nc.vector.tensor_tensor(
                    out=h_tok[h][:, cols, :].rearrange("p (c i) j -> p c j i", i=4),
                    in0=x_sb[:, h, :, cols].rearrange("p j (c i) -> p c j i", i=4),
                    in1=rg[:, h, :, cols].rearrange("p j (c i) -> p c j i", i=4),
                    op=ALU.mult)

        def quantize(pair, dtype, values):
            nc.vector.quantize_mx(out=pair[0][:].bitcast(dtype), scales=pair[1][:], in_=values)

        def qz(u):
            quantize(dz_tok_q[u], E5M2, dz_tok[u][:].rearrange("p c j -> p (c j)"))

        def qh(h):
            quantize(h_q[h], E4M3, h_tok[h][:].rearrange("p c j -> p (c j)"))

        def qt(u):
            quantize(dz_feat_q[u], E5M2, dz_feat[u][:].rearrange("p j q t -> p (j q t)"))

        def qw(u, h):
            quantize(w_q[u][h], E4M3, w_feat[u][h][:].rearrange("p c t -> p (c t)"))

        def tz(u, jp):
            bank = psum.tile([P, 4, P], F32, name="tr", tag="tr", bufs=3)
            words = dz_tok[u][:].rearrange("p c j -> p (c j)").bitcast(F32)
            for t in range(4):
                nc.tensor.transpose(bank[:, t, :], words[:, 2 * t + jp : 2 * UNIT : 8], identity[:])
            banks["z", u, jp] = bank

        def tw(u, h, ip):
            bank = psum.tile([P, 4, P], F32, name="tr", tag="tr", bufs=3)
            words = w_sb[u // 2][h][:].rearrange("p i f -> p (i f)").bitcast(F32)
            for i in range(2):
                first = (2 * ip + i) * (J // 2) + (u % 2) * (UNIT // 2)
                for s in range(2):
                    nc.tensor.transpose(bank[:, 2 * i + s, :], words[:, first + s : first + UNIT // 2 : 2], identity[:])
            banks["w", u, h, ip] = bank

        def dw(u, e):
            bank = psum.tile([P, UNIT], F32, name="dw", tag="dw", bufs=3)
            lhs, lhs_scale = h_q[e // 4]
            rhs, rhs_scale = dz_tok_q[u]
            cols = slice((e % 4) * P, (e % 4 + 1) * P)
            nc.tensor.matmul_mx(out=bank[:], lhsT=lhs[:, cols].bitcast(E4M3), lhsT_scale=lhs_scale[:, cols],
                                rhs=rhs[:].bitcast(E5M2), rhs_scale=rhs_scale[:], start=True, stop=True)
            banks["d", u, e] = bank

        def copy(on_vector, out, in_):
            if on_vector:
                nc.vector.tensor_copy(out=out, in_=in_)
            else:
                nc.scalar.copy(out=out, in_=in_)

        def cz(on_vector, u, jp):
            bank = banks["z", u, jp]
            copy(on_vector, dz_feat[u][:, 2 * jp : 2 * jp + 2],
                 bank[:].rearrange("p t q -> p (t q)").bitcast(BF16).rearrange("p (t q s) -> p s q t", t=4, s=2))

        def cw(on_vector, u, h, ip):
            bank = banks["w", u, h, ip]
            rows = w_feat[u][h][:].rearrange("p c t -> p (c t)").bitcast(F32).rearrange("p (q w) -> p q w", w=8)
            copy(on_vector, rows[:, :, 4 * ip : 4 * ip + 4], bank[:].rearrange("p w q -> p q w"))

        def cd(on_vector, u, e):
            tile = reused.tile([P, UNIT], F32, name="store", tag="store", bufs=8)
            copy(on_vector, tile[:], banks["d", u, e][:])
            nc.sync.dma_start(out=weight_grads[u // 2][e * P : (e + 1) * P, (u % 2) * UNIT : (u % 2 + 1) * UNIT], in_=tile[:])

        def dh(j, h):
            bank = psum.tile([P, HALF], F32, name="dh", tag="dh", bufs=2)
            cols = slice(j * P, (j + 1) * P)
            for u in range(UNITS):
                lhs, lhs_scale = dz_feat_q[u]
                rhs, rhs_scale = w_q[u][h]
                nc.tensor.matmul_mx(out=bank[:], lhsT=lhs[:, cols].bitcast(E5M2), lhsT_scale=lhs_scale[:, cols],
                                    rhs=rhs[:].bitcast(E4M3), rhs_scale=rhs_scale[:], start=(u == 0), stop=(u == UNITS - 1))
            banks["h", j, h] = bank

        def scale(j, h):
            nc.vector.tensor_tensor(out=scaled[j][:, h], in0=banks["h", j, h][:], in1=rg[:, h, j], op=ALU.mult)

        def dot(j):
            product = reused.tile([P, 2, HALF], F32, name="product", tag="product", bufs=2)
            nc.vector.scalar_tensor_tensor(product[:], x_sb[:, :, j], neg_r2[:, j : j + 1], scaled[j], ALU.mult, ALU.mult,
                                           accum_out=coef[j][:])

        def out(j, pieces):
            result = reused.tile([P, 2, HALF], F32, name="result", tag="result", bufs=2)
            for piece in pieces:
                nc.vector.scalar_tensor_tensor(result[:, piece], x_sb[:, piece, j], coef[j][:], scaled[j][:, piece], ALU.mult, ALU.add)
                nc.sync.dma_start(out=out_rows[:, j, piece], in_=result[:, piece])

        steps = {"dk": dk, "rope": rope, "norm": norm, "qz": qz, "qh": qh, "qt": qt, "qw": qw, "tz": tz, "tw": tw, "dw": dw,
                 "dh": dh, "rg": rg_step, "gain": scale, "dot": dot}
        copies = {"cz": cz, "cw": cw, "cd": cd}
        order = ORDER.split()
        for step in order:
            digits = [int(c) for c in step if c in "0123456789"]
            kind = [k for k in list(steps) + list(copies) + ["out"] if step.startswith(k)][0]
            if kind in copies:
                copies[kind](step[-1] == "v", *digits)
            elif kind == "out":
                out(digits[0], [slice(0, 1), slice(1, 2)] if step == order[-1] else [slice(0, 2)])
            else:
                steps[kind](*digits)
